import numpy as np
import ml_dtypes


def mxq(x, axis, fmt="e4m3"):
    dtype, down = {"e4m3": (ml_dtypes.float8_e4m3fn, 7), "e5m2": (ml_dtypes.float8_e5m2, 14)}[fmt]
    v = np.moveaxis(np.asarray(x, np.float32).astype(ml_dtypes.bfloat16).astype(np.float64), axis, -1)
    blocks = v.reshape(v.shape[:-1] + (-1, 32))
    amax = np.abs(blocks).max(-1, keepdims=True)
    byte = np.maximum(np.where(amax > 0, np.frexp(amax)[1] - 1 + 127, 0) - down, 1)
    scale = np.exp2(byte - 127.0)
    codes = (blocks / scale).astype(np.float32).astype(dtype).astype(np.float64)
    return np.moveaxis((codes * scale).reshape(v.shape), -1, axis)


WIDE = False


def mx_kscale(k):
    if not WIDE:
        return np.ones(k)
    levels = np.array([10, -10, 5, -5, 0])
    if k % 512:
        return np.exp2(np.random.permutation(np.resize(levels, k // 32))).repeat(32)
    a = np.empty((k // 512, 16))
    for p in range(k // 512):
        a[p, :8] = np.random.permutation(np.resize(levels, 8))
        for g in range(8):
            far = levels[np.abs(levels - a[p, g]) >= 10]
            a[p, g + 8] = far[np.random.randint(len(far))]
    return np.exp2(a.ravel()).repeat(32)


BF16 = ml_dtypes.bfloat16


def bf(x):
    return np.asarray(x, np.float32).astype(BF16)


def f64(x):
    return np.asarray(x).astype(np.float64)


N_FFT, B, T = 512, 16, 256
STRIDE = N_FFT + 1
L = T * STRIDE


def _fourier_kernels(n_fft):
    s = np.arange(n_fft, dtype=np.float64)
    k = np.arange(n_fft, dtype=np.float64)[:, None]
    ang = 2.0 * np.pi * k * s / n_fft
    return np.sin(ang), np.cos(ang)


def setup_inputs():
    s = mx_kscale(N_FFT)
    sx = np.concatenate([s, np.ones(1)])
    x = (np.random.standard_normal((1, B, T, STRIDE)) * sx).reshape(1, B, L)
    ws, wc = _fourier_kernels(N_FFT)
    wsin = (ws + 0.5 * np.random.standard_normal((N_FFT, N_FFT))) / np.sqrt(N_FFT) / s[None, :]
    wcos = (wc + 0.5 * np.random.standard_normal((N_FFT, N_FFT))) / np.sqrt(N_FFT) / s[None, :]
    return {"x": bf(x), "wsin": bf(wsin), "wcos": bf(wcos)}


def reference(x, wsin, wcos):
    sig = f64(x)[0]
    frames = sig.reshape(B, T, STRIDE)[..., :N_FFT]
    fq = mxq(frames, 2, "e4m3")
    real = np.einsum('btn,kn->tbk', fq, mxq(f64(wcos), 1, "e4m3"))
    imag = np.einsum('btn,kn->tbk', fq, mxq(f64(wsin), 1, "e4m3"))
    return real, -imag

@@ -1,0 +1,137 @@
+from contextlib import ExitStack
+
+import concourse.mybir as mybir
+from concourse.masks import make_identity
+
+F32 = mybir.dt.float32
+BF16 = mybir.dt.bfloat16
+U32 = mybir.dt.uint32
+U8 = mybir.dt.uint8
+FP8X4 = mybir.dt.float8_e4m3fn_x4
+
+P = 128
+N_FFT = 512
+SIGNALS = 16
+STRIDE = N_FFT + 1
+RUN = 2 * STRIDE
+RUN_PITCH = 1040
+PACK = 4
+WORDS = N_FFT // 2
+HALVES = WORDS // P
+GROUP = 4
+LOADS = SIGNALS // GROUP
+CHUNKS = 2 * LOADS
+
+FLOPS = 2 * SIGNALS * 2 * P * N_FFT * (2 * N_FFT)
+
+
+def quantise_group(nc, pools, rows, ident):
+    grouped = pools["grouped"].tile([P, GROUP * P * PACK], BF16, align_bytes=64)
+    grouped_words = grouped[:].bitcast(F32).rearrange("p (a r u) -> p a r u", a=GROUP, u=HALVES)
+    for pair in range(GROUP // 2):
+        flipped = pools["flipped"].tile([P, 2, HALVES, P], F32)
+        for a in range(2):
+            row_words = rows[:, 2 * pair + a, :].bitcast(F32)
+            for u in range(HALVES):
+                nc.tensor.transpose(flipped[:, a, u, :], row_words[:, u : WORDS : HALVES], ident[:])
+        nc.scalar.copy(
+            out=grouped_words[:, 2 * pair : 2 * pair + 2, :, :],
+            in_=flipped[:].rearrange("p a u r -> p a r u"),
+        )
+    codes = pools["codes"].tile([P, GROUP * P], U32, align_bytes=64)
+    scales = pools["scales"].tile([P, GROUP * P], U8, align_bytes=64)
+    nc.vector.quantize_mx(out=codes[:].bitcast(FP8X4), scales=scales[:], in_=grouped[:])
+    return codes, scales
+
+
+def multiply_group(nc, pools, frames, weight):
+    frame_codes, frame_scales = frames
+    weight_codes, weight_scales = weight
+    products = []
+    for a in range(GROUP):
+        cols = slice(a * P, (a + 1) * P)
+        product = pools["product"].tile([P, N_FFT], F32)
+        nc.tensor.matmul_mx(
+            out=product[:],
+            lhsT=frame_codes[:, cols].bitcast(FP8X4),
+            lhsT_scale=frame_scales[:, cols],
+            rhs=weight_codes[:].bitcast(FP8X4),
+            rhs_scale=weight_scales[:],
+            start=True,
+            stop=True,
+        )
+        products.append(product)
+    return products
+
+
+def tile_dftlayer_t_kernel(tc, x, wsin, wcos, out_0, out_1):
+    nc = tc.nc
+    with ExitStack() as ctx:
+        pools = {
+            "weights": ctx.enter_context(tc.tile_pool(name="weights", bufs=2)),
+            "runs": ctx.enter_context(tc.tile_pool(name="runs", bufs=LOADS)),
+            "odd": ctx.enter_context(tc.tile_pool(name="odd", bufs=LOADS)),
+            "const": ctx.enter_context(tc.tile_pool(name="const", bufs=1)),
+            "grouped": ctx.enter_context(tc.tile_pool(name="grouped", bufs=3)),
+            "codes": ctx.enter_context(tc.tile_pool(name="codes", bufs=2 + 3)),
+            "scales": ctx.enter_context(tc.tile_pool(name="scales", bufs=2 + 3)),
+            "results": ctx.enter_context(tc.tile_pool(name="results", bufs=CHUNKS)),
+            "flipped": ctx.enter_context(tc.psum_pool(name="flipped", bufs=2)),
+            "product": ctx.enter_context(tc.psum_pool(name="product", bufs=6)),
+        }
+        ctx.enter_context(tc.manual_schedule())
+
+        def load_weight(w):
+            w_rows = pools["weights"].tile([P, GROUP, N_FFT], BF16)
+            nc.sync.dma_start(out=w_rows[:], in_=w.rearrange("(a p) n -> p a n", p=P))
+            return w_rows
+
+        def load_runs(g):
+            runs = pools["runs"].tile([P, GROUP, RUN_PITCH], BF16)
+            nc.sync.dma_start(
+                out=runs[:, :, 0:RUN],
+                in_=x[0].rearrange("b (p s) -> p b s", s=RUN)[:, g * GROUP : (g + 1) * GROUP, :],
+            )
+            return runs
+
+        sin_rows = load_weight(wsin)
+        all_runs = [load_runs(0)]
+        cos_rows = load_weight(wcos)
+        for g in range(1, LOADS):
+            all_runs.append(load_runs(g))
+
+        ident = pools["const"].tile([P, P], F32)
+        make_identity(nc, ident[:])
+
+        chunk_rows = [runs[:, :, 0:N_FFT] for runs in all_runs]
+
+        sin_weight = quantise_group(nc, pools, sin_rows[:], ident)
+        frames = quantise_group(nc, pools, chunk_rows[0], ident)
+        cos_weight = quantise_group(nc, pools, cos_rows[:], ident)
+
+        real_view = out_0.rearrange("(p two) b k -> p two b k", two=2)
+        minus_imag_view = out_1.rearrange("(p two) b k -> p two b k", two=2)
+
+        for c in range(CHUNKS):
+            parity, g = c // LOADS, c % LOADS
+            signals = slice(g * GROUP, (g + 1) * GROUP)
+
+            sin_products = multiply_group(nc, pools, frames, sin_weight)
+            minus_imag = pools["results"].tile([P, GROUP, N_FFT], F32)
+            for a in range(GROUP):
+                nc.vector.tensor_scalar_mul(out=minus_imag[:, a, :], in0=sin_products[a][:], scalar1=-1.0)
+            nc.sync.dma_start(out=minus_imag_view[:, parity, signals, :], in_=minus_imag[:])
+
+            this_frames = frames
+            if c + 1 < CHUNKS:
+                frames = quantise_group(nc, pools, chunk_rows[c + 1], ident)
+            if parity == 0:
+                odd = pools["odd"].tile([P, GROUP, N_FFT], BF16)
+                nc.vector.tensor_copy(out=odd[:], in_=all_runs[g][:, :, STRIDE : STRIDE + N_FFT])
+                chunk_rows.append(odd[:])
+
+            cos_products = multiply_group(nc, pools, this_frames, cos_weight)
+            real = pools["results"].tile([P, GROUP, N_FFT], F32)
+            for a in range(GROUP):
+                nc.scalar.copy(out=real[:, a, :], in_=cos_products[a][:])
+            nc.sync.dma_start(out=real_view[:, parity, signals, :], in_=real[:])

@@ -19,27 +19,38 @@ PACK = 4
 WORDS = N_FFT // 2
 HALVES = WORDS // P
 GROUP = 4
-LOADS = SIGNALS // GROUP
-CHUNKS = 2 * LOADS
+GROUPS = SIGNALS // GROUP
+HEAD = 2
+CHUNKS = (
+    [(0, b, b + HEAD) for b in range(0, GROUP, HEAD)]
+    + [(0, b, b + GROUP) for b in range(GROUP, SIGNALS, GROUP)]
+    + [(1, b, b + GROUP) for b in range(0, SIGNALS, GROUP)]
+)
 
 FLOPS = 2 * SIGNALS * 2 * P * N_FFT * (2 * N_FFT)
 
 
-def quantise_group(nc, pools, rows, ident):
-    grouped = pools["grouped"].tile([P, GROUP * P * PACK], BF16, align_bytes=64)
-    grouped_words = grouped[:].bitcast(F32).rearrange("p (a r u) -> p a r u", a=GROUP, u=HALVES)
-    for pair in range(GROUP // 2):
-        flipped = pools["flipped"].tile([P, 2, HALVES, P], F32)
+def transpose_group(nc, pools, rows, ident, copies):
+    tiles = rows.shape[1]
+    grouped = pools["grouped"].tile([P, tiles * P * PACK], BF16, align_bytes=64)
+    grouped_words = grouped[:].bitcast(F32).rearrange("p (a r u) -> p a r u", a=tiles, u=HALVES)
+    for pair in range(tiles // 2):
+        flipped = pools["banks"].tile([P, 2, HALVES, P], F32, tag="bank")
         for a in range(2):
             row_words = rows[:, 2 * pair + a, :].bitcast(F32)
             for u in range(HALVES):
                 nc.tensor.transpose(flipped[:, a, u, :], row_words[:, u : WORDS : HALVES], ident[:])
-        nc.scalar.copy(
+        copies[pair](
             out=grouped_words[:, 2 * pair : 2 * pair + 2, :, :],
             in_=flipped[:].rearrange("p a u r -> p a r u"),
         )
-    codes = pools["codes"].tile([P, GROUP * P], U32, align_bytes=64)
-    scales = pools["scales"].tile([P, GROUP * P], U8, align_bytes=64)
+    return grouped
+
+
+def quantise_group(nc, pools, grouped):
+    width = grouped[:].shape[1] // PACK
+    codes = pools["codes"].tile([P, width], U32, align_bytes=64)
+    scales = pools["scales"].tile([P, width], U8, align_bytes=64)
     nc.vector.quantize_mx(out=codes[:].bitcast(FP8X4), scales=scales[:], in_=grouped[:])
     return codes, scales
 
@@ -48,9 +59,9 @@ def multiply_group(nc, pools, frames, weight):
     frame_codes, frame_scales = frames
     weight_codes, weight_scales = weight
     products = []
-    for a in range(GROUP):
+    for a in range(frame_codes.shape[1] // P):
         cols = slice(a * P, (a + 1) * P)
-        product = pools["product"].tile([P, N_FFT], F32)
+        product = pools["banks"].tile([P, N_FFT], F32, tag="bank")
         nc.tensor.matmul_mx(
             out=product[:],
             lhsT=frame_codes[:, cols].bitcast(FP8X4),
@@ -69,15 +80,14 @@ def tile_dftlayer_t_kernel(tc, x, wsin, wcos, out_0, out_1):
     with ExitStack() as ctx:
         pools = {
             "weights": ctx.enter_context(tc.tile_pool(name="weights", bufs=2)),
-            "runs": ctx.enter_context(tc.tile_pool(name="runs", bufs=LOADS)),
-            "odd": ctx.enter_context(tc.tile_pool(name="odd", bufs=LOADS)),
+            "runs": ctx.enter_context(tc.tile_pool(name="runs", bufs=GROUPS)),
+            "odd": ctx.enter_context(tc.tile_pool(name="odd", bufs=GROUPS)),
             "const": ctx.enter_context(tc.tile_pool(name="const", bufs=1)),
             "grouped": ctx.enter_context(tc.tile_pool(name="grouped", bufs=3)),
             "codes": ctx.enter_context(tc.tile_pool(name="codes", bufs=2 + 3)),
             "scales": ctx.enter_context(tc.tile_pool(name="scales", bufs=2 + 3)),
-            "results": ctx.enter_context(tc.tile_pool(name="results", bufs=CHUNKS)),
-            "flipped": ctx.enter_context(tc.psum_pool(name="flipped", bufs=2)),
-            "product": ctx.enter_context(tc.psum_pool(name="product", bufs=6)),
+            "results": ctx.enter_context(tc.tile_pool(name="results", bufs=len(CHUNKS))),
+            "banks": ctx.enter_context(tc.psum_pool(name="banks", bufs=8)),
         }
         ctx.enter_context(tc.manual_schedule())
 
@@ -86,52 +96,77 @@ def tile_dftlayer_t_kernel(tc, x, wsin, wcos, out_0, out_1):
             nc.sync.dma_start(out=w_rows[:], in_=w.rearrange("(a p) n -> p a n", p=P))
             return w_rows
 
-        def load_runs(g):
-            runs = pools["runs"].tile([P, GROUP, RUN_PITCH], BF16)
+        def load_runs(runs, first, last):
+            at = first % GROUP
             nc.sync.dma_start(
-                out=runs[:, :, 0:RUN],
-                in_=x[0].rearrange("b (p s) -> p b s", s=RUN)[:, g * GROUP : (g + 1) * GROUP, :],
+                out=runs[:, at : at + last - first, 0:RUN],
+                in_=x[0].rearrange("b (p s) -> p b s", s=RUN)[:, first:last, :],
             )
-            return runs
+
+        all_runs = []
+        for g in range(GROUPS):
+            runs = pools["runs"].tile([P, GROUP, RUN_PITCH], BF16)
+            all_runs.append(runs)
 
         sin_rows = load_weight(wsin)
-        all_runs = [load_runs(0)]
         cos_rows = load_weight(wcos)
-        for g in range(1, LOADS):
-            all_runs.append(load_runs(g))
+        for b in range(0, GROUP, HEAD):
+            load_runs(all_runs[0], b, b + HEAD)
+        for g in range(1, GROUPS):
+            load_runs(all_runs[g], g * GROUP, (g + 1) * GROUP)
 
         ident = pools["const"].tile([P, P], F32)
         make_identity(nc, ident[:])
 
-        chunk_rows = [runs[:, :, 0:N_FFT] for runs in all_runs]
+        def even_rows(first, last):
+            at = first % GROUP
+            return all_runs[first // GROUP][:, at : at + last - first, 0:N_FFT]
 
-        sin_weight = quantise_group(nc, pools, sin_rows[:], ident)
-        frames = quantise_group(nc, pools, chunk_rows[0], ident)
-        cos_weight = quantise_group(nc, pools, cos_rows[:], ident)
+        odd_rows = []
+
+        def chunk_rows(c):
+            parity, first, last = CHUNKS[c]
+            return odd_rows[first // GROUP][:] if parity else even_rows(first, last)
+
+        both = [nc.scalar.copy, nc.vector.tensor_copy]
+        sin_weight = quantise_group(nc, pools, transpose_group(nc, pools, sin_rows[:], ident, both))
+        cos_weight = quantise_group(nc, pools, transpose_group(nc, pools, cos_rows[:], ident, both))
+
+        def transpose_chunk(c):
+            rows = chunk_rows(c)
+            return transpose_group(nc, pools, rows, ident, [nc.scalar.copy] * (rows.shape[1] // 2))
+
+        grouped = {}
+        frames = {}
+        for c in range(2):
+            grouped[c] = transpose_chunk(c)
+            frames[c] = quantise_group(nc, pools, grouped[c])
 
         real_view = out_0.rearrange("(p two) b k -> p two b k", two=2)
         minus_imag_view = out_1.rearrange("(p two) b k -> p two b k", two=2)
 
-        for c in range(CHUNKS):
-            parity, g = c // LOADS, c % LOADS
-            signals = slice(g * GROUP, (g + 1) * GROUP)
+        for c in range(len(CHUNKS)):
+            parity, first, last = CHUNKS[c]
+            tiles = last - first
 
-            sin_products = multiply_group(nc, pools, frames, sin_weight)
-            minus_imag = pools["results"].tile([P, GROUP, N_FFT], F32)
-            for a in range(GROUP):
+            sin_products = multiply_group(nc, pools, frames[c], sin_weight)
+            minus_imag = pools["results"].tile([P, tiles, N_FFT], F32)
+            for a in range(tiles):
                 nc.vector.tensor_scalar_mul(out=minus_imag[:, a, :], in0=sin_products[a][:], scalar1=-1.0)
-            nc.sync.dma_start(out=minus_imag_view[:, parity, signals, :], in_=minus_imag[:])
+            nc.sync.dma_start(out=minus_imag_view[:, parity, first:last, :], in_=minus_imag[:])
 
-            this_frames = frames
-            if c + 1 < CHUNKS:
-                frames = quantise_group(nc, pools, chunk_rows[c + 1], ident)
-            if parity == 0:
+            cos_products = multiply_group(nc, pools, frames[c], cos_weight)
+            real = pools["results"].tile([P, tiles, N_FFT], F32)
+            for a in range(tiles):
+                nc.scalar.copy(out=real[:, a, :], in_=cos_products[a][:])
+            nc.sync.dma_start(out=real_view[:, parity, first:last, :], in_=real[:])
+
+            if 1 <= c and c + 1 < len(CHUNKS):
+                frames[c + 1] = quantise_group(nc, pools, grouped[c + 1])
+            g = c - 2
+            if 0 <= g < GROUPS:
                 odd = pools["odd"].tile([P, GROUP, N_FFT], BF16)
                 nc.vector.tensor_copy(out=odd[:], in_=all_runs[g][:, :, STRIDE : STRIDE + N_FFT])
-                chunk_rows.append(odd[:])
-
-            cos_products = multiply_group(nc, pools, this_frames, cos_weight)
-            real = pools["results"].tile([P, GROUP, N_FFT], F32)
-            for a in range(GROUP):
-                nc.scalar.copy(out=real[:, a, :], in_=cos_products[a][:])
-            nc.sync.dma_start(out=real_view[:, parity, signals, :], in_=real[:])
+                odd_rows.append(odd)
+            if c + 2 < len(CHUNKS):
+                grouped[c + 2] = transpose_chunk(c + 2)

@@ -30,20 +30,21 @@ CHUNKS = (
 FLOPS = 2 * SIGNALS * 2 * P * N_FFT * (2 * N_FFT)
 
 
-def transpose_group(nc, pools, rows, ident, copies):
+def transpose_group(nc, pools, rows, ident, copies, interleave):
     tiles = rows.shape[1]
     grouped = pools["grouped"].tile([P, tiles * P * PACK], BF16, align_bytes=64)
-    grouped_words = grouped[:].bitcast(F32).rearrange("p (a r u) -> p a r u", a=tiles, u=HALVES)
+    if interleave:
+        grouped_words = grouped[:].bitcast(F32).rearrange("p (r q v) -> p q r v", r=P, q=tiles // 2)
+    else:
+        grouped_words = grouped[:].bitcast(F32).rearrange("p (q a r u) -> p q a r u", a=2, r=P, u=HALVES)
     for pair in range(tiles // 2):
         flipped = pools["banks"].tile([P, 2, HALVES, P], F32, tag="bank")
         for a in range(2):
             row_words = rows[:, 2 * pair + a, :].bitcast(F32)
             for u in range(HALVES):
                 nc.tensor.transpose(flipped[:, a, u, :], row_words[:, u : WORDS : HALVES], ident[:])
-        copies[pair](
-            out=grouped_words[:, 2 * pair : 2 * pair + 2, :, :],
-            in_=flipped[:].rearrange("p a u r -> p a r u"),
-        )
+        pattern = "p a u r -> p r (a u)" if interleave else "p a u r -> p a r u"
+        copies[pair](out=grouped_words[:, pair], in_=flipped[:].rearrange(pattern))
     return grouped
 
 
@@ -93,7 +94,7 @@ def tile_dftlayer_t_kernel(tc, x, wsin, wcos, out_0, out_1):
 
         def load_weight(w):
             w_rows = pools["weights"].tile([P, GROUP, N_FFT], BF16)
-            nc.sync.dma_start(out=w_rows[:], in_=w.rearrange("(a p) n -> p a n", p=P))
+            nc.sync.dma_start(out=w_rows[:], in_=w.rearrange("(p a) n -> p a n", p=P))
             return w_rows
 
         def load_runs(runs, first, last):
@@ -129,12 +130,12 @@ def tile_dftlayer_t_kernel(tc, x, wsin, wcos, out_0, out_1):
             return odd_rows[first // GROUP][:] if parity else even_rows(first, last)
 
         both = [nc.scalar.copy, nc.vector.tensor_copy]
-        sin_weight = quantise_group(nc, pools, transpose_group(nc, pools, sin_rows[:], ident, both))
-        cos_weight = quantise_group(nc, pools, transpose_group(nc, pools, cos_rows[:], ident, both))
+        sin_weight = quantise_group(nc, pools, transpose_group(nc, pools, sin_rows[:], ident, both, True))
+        cos_weight = quantise_group(nc, pools, transpose_group(nc, pools, cos_rows[:], ident, both, True))
 
         def transpose_chunk(c):
             rows = chunk_rows(c)
-            return transpose_group(nc, pools, rows, ident, [nc.scalar.copy] * (rows.shape[1] // 2))
+            return transpose_group(nc, pools, rows, ident, [nc.scalar.copy] * (rows.shape[1] // 2), False)
 
         grouped = {}
         frames = {}

@@ -13,18 +13,19 @@ P = 128
 N_FFT = 512
 SIGNALS = 16
 STRIDE = N_FFT + 1
-RUN = 2 * STRIDE
-RUN_PITCH = 1040
+TIMES = 4
+RUN = TIMES * STRIDE
+RUN_PITCH = 2064
+SLOTS = 8
 PACK = 4
 WORDS = N_FFT // 2
 HALVES = WORDS // P
 GROUP = 4
-GROUPS = SIGNALS // GROUP
 HEAD = 2
 CHUNKS = (
-    [(0, b, b + HEAD) for b in range(0, GROUP, HEAD)]
-    + [(0, b, b + GROUP) for b in range(GROUP, SIGNALS, GROUP)]
-    + [(1, b, b + GROUP) for b in range(0, SIGNALS, GROUP)]
+    [(j, i, i + HEAD) for i in range(0, GROUP, HEAD) for j in range(0, TIMES, 2)]
+    + [(j, GROUP, SLOTS) for j in range(0, TIMES, 2)]
+    + [(j, i, i + GROUP) for j in range(1, TIMES, 2) for i in range(0, SLOTS, GROUP)]
 )
 
 FLOPS = 2 * SIGNALS * 2 * P * N_FFT * (2 * N_FFT)
@@ -81,13 +82,13 @@ def tile_dftlayer_t_kernel(tc, x, wsin, wcos, out_0, out_1):
     with ExitStack() as ctx:
         pools = {
             "weights": ctx.enter_context(tc.tile_pool(name="weights", bufs=2)),
-            "runs": ctx.enter_context(tc.tile_pool(name="runs", bufs=GROUPS)),
-            "odd": ctx.enter_context(tc.tile_pool(name="odd", bufs=GROUPS)),
+            "runs": ctx.enter_context(tc.tile_pool(name="runs", bufs=1)),
+            "odd": ctx.enter_context(tc.tile_pool(name="odd", bufs=4)),
             "const": ctx.enter_context(tc.tile_pool(name="const", bufs=1)),
             "grouped": ctx.enter_context(tc.tile_pool(name="grouped", bufs=3)),
             "codes": ctx.enter_context(tc.tile_pool(name="codes", bufs=2 + 3)),
             "scales": ctx.enter_context(tc.tile_pool(name="scales", bufs=2 + 3)),
-            "results": ctx.enter_context(tc.tile_pool(name="results", bufs=len(CHUNKS))),
+            "results": ctx.enter_context(tc.tile_pool(name="results", bufs=1)),
             "banks": ctx.enter_context(tc.psum_pool(name="banks", bufs=8)),
         }
         ctx.enter_context(tc.manual_schedule())
@@ -97,37 +98,23 @@ def tile_dftlayer_t_kernel(tc, x, wsin, wcos, out_0, out_1):
             nc.sync.dma_start(out=w_rows[:], in_=w.rearrange("(p a) n -> p a n", p=P))
             return w_rows
 
-        def load_runs(runs, first, last):
-            at = first % GROUP
-            nc.sync.dma_start(
-                out=runs[:, at : at + last - first, 0:RUN],
-                in_=x[0].rearrange("b (p s) -> p b s", s=RUN)[:, first:last, :],
-            )
-
-        all_runs = []
-        for g in range(GROUPS):
-            runs = pools["runs"].tile([P, GROUP, RUN_PITCH], BF16)
-            all_runs.append(runs)
-
         sin_rows = load_weight(wsin)
         cos_rows = load_weight(wcos)
-        for b in range(0, GROUP, HEAD):
-            load_runs(all_runs[0], b, b + HEAD)
-        for g in range(1, GROUPS):
-            load_runs(all_runs[g], g * GROUP, (g + 1) * GROUP)
+        x_view = x[0].rearrange("(h i) (q s) -> i q h s", i=SLOTS, s=RUN)
+        runs = pools["runs"].tile([P, SLOTS, RUN_PITCH], BF16)
+        for i in range(SLOTS):
+            nc.sync.dma_start(out=runs[:, i, 0:RUN], in_=x_view[i])
 
         ident = pools["const"].tile([P, P], F32)
         make_identity(nc, ident[:])
 
-        def even_rows(first, last):
-            at = first % GROUP
-            return all_runs[first // GROUP][:, at : at + last - first, 0:N_FFT]
-
-        odd_rows = []
+        odd_rows = {}
 
         def chunk_rows(c):
-            parity, first, last = CHUNKS[c]
-            return odd_rows[first // GROUP][:] if parity else even_rows(first, last)
+            j, first, last = CHUNKS[c]
+            if j % 2:
+                return odd_rows[j, first][:]
+            return runs[:, first:last, j * STRIDE : j * STRIDE + N_FFT]
 
         both = [nc.scalar.copy, nc.vector.tensor_copy]
         sin_weight = quantise_group(nc, pools, transpose_group(nc, pools, sin_rows[:], ident, both, True))
@@ -143,31 +130,32 @@ def tile_dftlayer_t_kernel(tc, x, wsin, wcos, out_0, out_1):
             grouped[c] = transpose_chunk(c)
             frames[c] = quantise_group(nc, pools, grouped[c])
 
-        real_view = out_0.rearrange("(p two) b k -> p two b k", two=2)
-        minus_imag_view = out_1.rearrange("(p two) b k -> p two b k", two=2)
+        minus_imag = pools["results"].tile([P, TIMES, SLOTS, N_FFT], F32)
+        real = pools["results"].tile([P, TIMES, SLOTS, N_FFT], F32)
+
+        def store(out, result, j, first, last):
+            view = out.rearrange("(q j) (h i) k -> j q h i k", j=TIMES, i=SLOTS)
+            nc.sync.dma_start(out=view[j, :, :, first:last, :], in_=result[:, j, first:last, :])
 
         for c in range(len(CHUNKS)):
-            parity, first, last = CHUNKS[c]
-            tiles = last - first
+            j, first, last = CHUNKS[c]
 
             sin_products = multiply_group(nc, pools, frames[c], sin_weight)
-            minus_imag = pools["results"].tile([P, tiles, N_FFT], F32)
-            for a in range(tiles):
-                nc.vector.tensor_scalar_mul(out=minus_imag[:, a, :], in0=sin_products[a][:], scalar1=-1.0)
-            nc.sync.dma_start(out=minus_imag_view[:, parity, first:last, :], in_=minus_imag[:])
+            for a in range(last - first):
+                nc.vector.tensor_scalar_mul(out=minus_imag[:, j, first + a, :], in0=sin_products[a][:], scalar1=-1.0)
+            store(out_1, minus_imag, j, first, last)
 
             cos_products = multiply_group(nc, pools, frames[c], cos_weight)
-            real = pools["results"].tile([P, tiles, N_FFT], F32)
-            for a in range(tiles):
-                nc.scalar.copy(out=real[:, a, :], in_=cos_products[a][:])
-            nc.sync.dma_start(out=real_view[:, parity, first:last, :], in_=real[:])
+            for a in range(last - first):
+                nc.scalar.copy(out=real[:, j, first + a, :], in_=cos_products[a][:])
+            store(out_0, real, j, first, last)
 
             if 1 <= c and c + 1 < len(CHUNKS):
                 frames[c + 1] = quantise_group(nc, pools, grouped[c + 1])
-            g = c - 2
-            if 0 <= g < GROUPS:
+            if c + 3 < len(CHUNKS) and CHUNKS[c + 3][0] % 2:
+                j, first, last = CHUNKS[c + 3]
                 odd = pools["odd"].tile([P, GROUP, N_FFT], BF16)
-                nc.vector.tensor_copy(out=odd[:], in_=all_runs[g][:, :, STRIDE : STRIDE + N_FFT])
-                odd_rows.append(odd)
+                nc.vector.tensor_copy(out=odd[:], in_=runs[:, first:last, j * STRIDE : j * STRIDE + N_FFT])
+                odd_rows[j, first] = odd
             if c + 2 < len(CHUNKS):
                 grouped[c + 2] = transpose_chunk(c + 2)

@@ -15,7 +15,8 @@ SIGNALS = 16
 STRIDE = N_FFT + 1
 TIMES = 4
 RUN = TIMES * STRIDE
-RUN_PITCH = 2064
+BURST = 256
+RUN_PITCH = 2176
 SLOTS = 8
 PACK = 4
 WORDS = N_FFT // 2
@@ -94,14 +95,14 @@ def tile_dftlayer_t_kernel(tc, x, wsin, wcos, out_0, out_1):
         ctx.enter_context(tc.manual_schedule())
 
         def load_weight(w):
-            w_rows = pools["weights"].tile([P, GROUP, N_FFT], BF16)
+            w_rows = pools["weights"].tile([P, GROUP, N_FFT], BF16, align_bytes=BURST)
             nc.sync.dma_start(out=w_rows[:], in_=w.rearrange("(p a) n -> p a n", p=P))
             return w_rows
 
         sin_rows = load_weight(wsin)
         cos_rows = load_weight(wcos)
         x_view = x[0].rearrange("(h i) (q s) -> i q h s", i=SLOTS, s=RUN)
-        runs = pools["runs"].tile([P, SLOTS, RUN_PITCH], BF16)
+        runs = pools["runs"].tile([P, SLOTS, RUN_PITCH], BF16, align_bytes=BURST)
         for i in range(SLOTS):
             nc.sync.dma_start(out=runs[:, i, 0:RUN], in_=x_view[i])
 
@@ -130,8 +131,8 @@ def tile_dftlayer_t_kernel(tc, x, wsin, wcos, out_0, out_1):
             grouped[c] = transpose_chunk(c)
             frames[c] = quantise_group(nc, pools, grouped[c])
 
-        minus_imag = pools["results"].tile([P, TIMES, SLOTS, N_FFT], F32)
-        real = pools["results"].tile([P, TIMES, SLOTS, N_FFT], F32)
+        minus_imag = pools["results"].tile([P, TIMES, SLOTS, N_FFT], F32, align_bytes=BURST)
+        real = pools["results"].tile([P, TIMES, SLOTS, N_FFT], F32, align_bytes=BURST)
 
         def store(out, result, j, first, last):
             view = out.rearrange("(q j) (h i) k -> j q h i k", j=TIMES, i=SLOTS)

@@ -141,18 +141,14 @@ def tile_dftlayer_t_kernel(tc, x, wsin, wcos, out_0, out_1):
         for c in range(len(CHUNKS)):
             j, first, last = CHUNKS[c]
 
-            sin_products = multiply_group(nc, pools, frames[c], sin_weight)
-            for a in range(last - first):
-                nc.vector.tensor_scalar_mul(out=minus_imag[:, j, first + a, :], in0=sin_products[a][:], scalar1=-1.0)
-            store(out_1, minus_imag, j, first, last)
-
-            cos_products = multiply_group(nc, pools, frames[c], cos_weight)
-            for a in range(last - first):
-                nc.scalar.copy(out=real[:, j, first + a, :], in_=cos_products[a][:])
-            store(out_0, real, j, first, last)
-
-            if 1 <= c and c + 1 < len(CHUNKS):
-                frames[c + 1] = quantise_group(nc, pools, grouped[c + 1])
+            for weight, result, out, sign in ((sin_weight, minus_imag, out_1, -1.0), (cos_weight, real, out_0, 1.0)):
+                products = multiply_group(nc, pools, frames[c], weight)
+                for a in range(0, last - first, 2):
+                    nc.vector.tensor_scalar_mul(out=result[:, j, first + a, :], in0=products[a][:], scalar1=sign)
+                    nc.scalar.mul(result[:, j, first + a + 1, :], products[a + 1][:], sign)
+                store(out, result, j, first, last)
+                if c + 1 < len(CHUNKS) and c + 1 not in frames:
+                    frames[c + 1] = quantise_group(nc, pools, grouped[c + 1])
             if c + 3 < len(CHUNKS) and CHUNKS[c + 3][0] % 2:
                 j, first, last = CHUNKS[c + 3]
                 odd = pools["odd"].tile([P, GROUP, N_FFT], BF16)

@@ -13,21 +13,21 @@ P = 128
 N_FFT = 512
 SIGNALS = 16
 STRIDE = N_FFT + 1
-TIMES = 4
+TIMES = 8
 RUN = TIMES * STRIDE
 BURST = 256
-RUN_PITCH = 2176
-SLOTS = 8
+RUN_PITCH = 4224
+FIRST_PART = 2064
+SLOTS = 4
+QUARTERS = 4
 PACK = 4
 WORDS = N_FFT // 2
 HALVES = WORDS // P
 GROUP = 4
 HEAD = 2
-CHUNKS = (
-    [(j, i, i + HEAD) for i in range(0, GROUP, HEAD) for j in range(0, TIMES, 2)]
-    + [(j, GROUP, SLOTS) for j in range(0, TIMES, 2)]
-    + [(j, i, i + GROUP) for j in range(1, TIMES, 2) for i in range(0, SLOTS, GROUP)]
-)
+CHUNKS = [(j, i, i + HEAD) for i in range(0, SLOTS, HEAD) for j in range(0, TIMES, 2)] + [
+    (j, 0, SLOTS) for j in range(1, TIMES, 2)
+]
 
 FLOPS = 2 * SIGNALS * 2 * P * N_FFT * (2 * N_FFT)
 
@@ -103,8 +103,13 @@ def tile_dftlayer_t_kernel(tc, x, wsin, wcos, out_0, out_1):
         cos_rows = load_weight(wcos)
         x_view = x[0].rearrange("(h i) (q s) -> i q h s", i=SLOTS, s=RUN)
         runs = pools["runs"].tile([P, SLOTS, RUN_PITCH], BF16, align_bytes=BURST)
-        for i in range(SLOTS):
-            nc.sync.dma_start(out=runs[:, i, 0:RUN], in_=x_view[i])
+        pieces = (
+            [(i, 0, FIRST_PART) for i in range(HEAD)]
+            + [(i, FIRST_PART, RUN) for i in range(HEAD)]
+            + [(i, 0, RUN) for i in range(HEAD, SLOTS)]
+        )
+        for i, start, stop in pieces:
+            nc.sync.dma_start(out=runs[:, i, start:stop], in_=x_view[i, :, :, start:stop])
 
         ident = pools["const"].tile([P, P], F32)
         make_identity(nc, ident[:])

from contextlib import ExitStack

import concourse.mybir as mybir
from concourse.masks import make_identity

F32 = mybir.dt.float32
BF16 = mybir.dt.bfloat16
U32 = mybir.dt.uint32
U8 = mybir.dt.uint8
FP8X4 = mybir.dt.float8_e4m3fn_x4

P = 128
N_FFT = 512
SIGNALS = 16
STRIDE = N_FFT + 1
TIMES = 8
RUN = TIMES * STRIDE
BURST = 256
RUN_PITCH = 4224
FIRST_PART = 2064
SLOTS = 4
QUARTERS = 4
PACK = 4
WORDS = N_FFT // 2
HALVES = WORDS // P
GROUP = 4
HEAD = 2
CHUNKS = [(j, i, i + HEAD) for i in range(0, SLOTS, HEAD) for j in range(0, TIMES, 2)] + [
    (j, 0, SLOTS) for j in range(1, TIMES, 2)
]

FLOPS = 2 * SIGNALS * 2 * P * N_FFT * (2 * N_FFT)


def transpose_group(nc, pools, rows, ident, copies, interleave):
    tiles = rows.shape[1]
    grouped = pools["grouped"].tile([P, tiles * P * PACK], BF16, align_bytes=64)
    if interleave:
        grouped_words = grouped[:].bitcast(F32).rearrange("p (r q v) -> p q r v", r=P, q=tiles // 2)
    else:
        grouped_words = grouped[:].bitcast(F32).rearrange("p (q a r u) -> p q a r u", a=2, r=P, u=HALVES)
    for pair in range(tiles // 2):
        flipped = pools["banks"].tile([P, 2, HALVES, P], F32, tag="bank")
        for a in range(2):
            row_words = rows[:, 2 * pair + a, :].bitcast(F32)
            for u in range(HALVES):
                nc.tensor.transpose(flipped[:, a, u, :], row_words[:, u : WORDS : HALVES], ident[:])
        pattern = "p a u r -> p r (a u)" if interleave else "p a u r -> p a r u"
        copies[pair](out=grouped_words[:, pair], in_=flipped[:].rearrange(pattern))
    return grouped


def quantise_group(nc, pools, grouped):
    width = grouped[:].shape[1] // PACK
    codes = pools["codes"].tile([P, width], U32, align_bytes=64)
    scales = pools["scales"].tile([P, width], U8, align_bytes=64)
    nc.vector.quantize_mx(out=codes[:].bitcast(FP8X4), scales=scales[:], in_=grouped[:])
    return codes, scales


def multiply_group(nc, pools, frames, weight):
    frame_codes, frame_scales = frames
    weight_codes, weight_scales = weight
    products = []
    for a in range(frame_codes.shape[1] // P):
        cols = slice(a * P, (a + 1) * P)
        product = pools["banks"].tile([P, N_FFT], F32, tag="bank")
        nc.tensor.matmul_mx(
            out=product[:],
            lhsT=frame_codes[:, cols].bitcast(FP8X4),
            lhsT_scale=frame_scales[:, cols],
            rhs=weight_codes[:].bitcast(FP8X4),
            rhs_scale=weight_scales[:],
            start=True,
            stop=True,
        )
        products.append(product)
    return products


def tile_dftlayer_t_kernel(tc, x, wsin, wcos, out_0, out_1):
    nc = tc.nc
    with ExitStack() as ctx:
        pools = {
            "weights": ctx.enter_context(tc.tile_pool(name="weights", bufs=2)),
            "runs": ctx.enter_context(tc.tile_pool(name="runs", bufs=1)),
            "odd": ctx.enter_context(tc.tile_pool(name="odd", bufs=4)),
            "const": ctx.enter_context(tc.tile_pool(name="const", bufs=1)),
            "grouped": ctx.enter_context(tc.tile_pool(name="grouped", bufs=3)),
            "codes": ctx.enter_context(tc.tile_pool(name="codes", bufs=2 + 3)),
            "scales": ctx.enter_context(tc.tile_pool(name="scales", bufs=2 + 3)),
            "results": ctx.enter_context(tc.tile_pool(name="results", bufs=1)),
            "banks": ctx.enter_context(tc.psum_pool(name="banks", bufs=8)),
        }
        ctx.enter_context(tc.manual_schedule())

        def load_weight(w):
            w_rows = pools["weights"].tile([P, GROUP, N_FFT], BF16, align_bytes=BURST)
            nc.sync.dma_start(out=w_rows[:], in_=w.rearrange("(p a) n -> p a n", p=P))
            return w_rows

        sin_rows = load_weight(wsin)
        cos_rows = load_weight(wcos)
        x_view = x[0].rearrange("(h i) (q s) -> i q h s", i=SLOTS, s=RUN)
        runs = pools["runs"].tile([P, SLOTS, RUN_PITCH], BF16, align_bytes=BURST)
        pieces = (
            [(i, 0, FIRST_PART) for i in range(HEAD)]
            + [(i, FIRST_PART, RUN) for i in range(HEAD)]
            + [(i, 0, RUN) for i in range(HEAD, SLOTS)]
        )
        for i, start, stop in pieces:
            nc.sync.dma_start(out=runs[:, i, start:stop], in_=x_view[i, :, :, start:stop])

        ident = pools["const"].tile([P, P], F32)
        make_identity(nc, ident[:])

        odd_rows = {}

        def chunk_rows(c):
            j, first, last = CHUNKS[c]
            if j % 2:
                return odd_rows[j, first][:]
            return runs[:, first:last, j * STRIDE : j * STRIDE + N_FFT]

        both = [nc.scalar.copy, nc.vector.tensor_copy]
        sin_weight = quantise_group(nc, pools, transpose_group(nc, pools, sin_rows[:], ident, both, True))
        cos_weight = quantise_group(nc, pools, transpose_group(nc, pools, cos_rows[:], ident, both, True))

        def transpose_chunk(c):
            rows = chunk_rows(c)
            return transpose_group(nc, pools, rows, ident, [nc.scalar.copy] * (rows.shape[1] // 2), False)

        grouped = {}
        frames = {}
        for c in range(2):
            grouped[c] = transpose_chunk(c)
            frames[c] = quantise_group(nc, pools, grouped[c])

        minus_imag = pools["results"].tile([P, TIMES, SLOTS, N_FFT], F32, align_bytes=BURST)
        real = pools["results"].tile([P, TIMES, SLOTS, N_FFT], F32, align_bytes=BURST)

        def store(out, result, j, first, last):
            view = out.rearrange("(q j) (h i) k -> j q h i k", j=TIMES, i=SLOTS)
            nc.sync.dma_start(out=view[j, :, :, first:last, :], in_=result[:, j, first:last, :])

        for c in range(len(CHUNKS)):
            j, first, last = CHUNKS[c]

            for weight, result, out, sign in ((sin_weight, minus_imag, out_1, -1.0), (cos_weight, real, out_0, 1.0)):
                products = multiply_group(nc, pools, frames[c], weight)
                for a in range(0, last - first, 2):
                    nc.vector.tensor_scalar_mul(out=result[:, j, first + a, :], in0=products[a][:], scalar1=sign)
                    nc.scalar.mul(result[:, j, first + a + 1, :], products[a + 1][:], sign)
                store(out, result, j, first, last)
                if c + 1 < len(CHUNKS) and c + 1 not in frames:
                    frames[c + 1] = quantise_group(nc, pools, grouped[c + 1])
            if c + 3 < len(CHUNKS) and CHUNKS[c + 3][0] % 2:
                j, first, last = CHUNKS[c + 3]
                odd = pools["odd"].tile([P, GROUP, N_FFT], BF16)
                nc.vector.tensor_copy(out=odd[:], in_=runs[:, first:last, j * STRIDE : j * STRIDE + N_FFT])
                odd_rows[j, first] = odd
            if c + 2 < len(CHUNKS):
                grouped[c + 2] = transpose_chunk(c + 2)
